import numpy as np
import ml_dtypes


def mxq(x, axis, fmt="e4m3"):
    dtype, down = {"e4m3": (ml_dtypes.float8_e4m3fn, 7), "e5m2": (ml_dtypes.float8_e5m2, 14)}[fmt]
    v = np.moveaxis(np.asarray(x, np.float32).astype(ml_dtypes.bfloat16).astype(np.float64), axis, -1)
    blocks = v.reshape(v.shape[:-1] + (-1, 32))
    amax = np.abs(blocks).max(-1, keepdims=True)
    byte = np.maximum(np.where(amax > 0, np.frexp(amax)[1] - 1 + 127, 0) - down, 1)
    scale = np.exp2(byte - 127.0)
    codes = (blocks / scale).astype(np.float32).astype(dtype).astype(np.float64)
    return np.moveaxis((codes * scale).reshape(v.shape), -1, axis)


WIDE = False


def mx_kscale(k):
    if not WIDE:
        return np.ones(k)
    levels = np.array([10, -10, 5, -5, 0])
    if k % 512:
        return np.exp2(np.random.permutation(np.resize(levels, k // 32))).repeat(32)
    a = np.empty((k // 512, 16))
    for p in range(k // 512):
        a[p, :8] = np.random.permutation(np.resize(levels, 8))
        for g in range(8):
            far = levels[np.abs(levels - a[p, g]) >= 10]
            a[p, g + 8] = far[np.random.randint(len(far))]
    return np.exp2(a.ravel()).repeat(32)


BF16 = ml_dtypes.bfloat16


def bf(x):
    return np.asarray(x, np.float32).astype(BF16)


def f64(x):
    return np.asarray(x).astype(np.float64)


T, B, H, DH, R, L = 128, 2, 16, 128, 64, 512
M = H * DH


def rope_tables():
    inv_freq = 1.0 / (10000.0 ** (f64(np.arange(0, R, 2)) / R))
    pos = f64(np.arange(L))
    ang = pos[:, None] * inv_freq[None, :]
    sin = np.repeat(np.sin(ang), 2, axis=-1)[-T:]
    cos = np.repeat(np.cos(ang), 2, axis=-1)[-T:]
    return sin[:, None, None, :], cos[:, None, None, :]


def rotate_every_two(u):
    return np.stack((-u[..., 1::2], u[..., ::2]), axis=-1).reshape(u.shape)


def apply_rope(u):
    sin, cos = rope_tables()
    u_rot = u[..., :R]
    u_pass = u[..., R:]
    u_rot = u_rot * cos + rotate_every_two(u_rot) * sin
    return np.concatenate([u_rot, u_pass], axis=-1)


def draw0():
    s = mx_kscale(M)
    return {"x": bf(np.random.standard_normal((T, B, M)) * s),
            "in_proj_weight": bf(np.random.standard_normal((3 * M, M)) / np.sqrt(M) / s[None, :]),
            "in_proj_bias": bf(np.random.standard_normal(3 * M) * 0.3)}


def core(x, in_proj_weight, in_proj_bias):
    all_out = (mxq(f64(x), 2, "e4m3") @ mxq(f64(in_proj_weight), 1, "e4m3").T) + f64(in_proj_bias)
    q, k, v = np.split(all_out, 3, axis=-1)
    qh = q.reshape(T, B, H, DH)
    kh = k.reshape(T, B, H, DH)
    vh = v.reshape(T, B, H, DH)
    return apply_rope(qh), apply_rope(kh), vh


def e4m3fn_bytes(y):
    return np.clip(np.asarray(y, np.float64), -448.0, 448.0).astype(np.float32).astype(ml_dtypes.float8_e4m3fn).view(np.uint8)


def e4m3fn_values(b):
    return np.asarray(b, np.uint8).view(ml_dtypes.float8_e4m3fn).astype(np.float64)


def setup_inputs():
    d = draw0()
    x0 = np.asarray(d['in_proj_weight']).astype(np.float64)
    s = (np.max(np.abs(x0), axis=(0,), keepdims=True) / 448.0).astype(np.float32)
    out = {}
    for k, v in d.items():
        if k == 'in_proj_weight':
            out['in_proj_weight_bytes'] = e4m3fn_bytes(x0 / s.astype(np.float64))
            out['in_proj_weight_scale'] = s
        else:
            out[k] = v
    return out


def reference(x, in_proj_weight_bytes, in_proj_weight_scale, in_proj_bias):
    return core(x, e4m3fn_values(in_proj_weight_bytes) * in_proj_weight_scale.astype(np.float64), in_proj_bias)

@@ -1,0 +1,352 @@
+from contextlib import ExitStack
+
+import concourse.mybir as mybir
+from concourse.masks import make_identity
+
+T, B, H, DH, R = 128, 2, 16, 128, 64
+M = H * DH
+NH = 3 * H
+P = 128
+G = 4
+NP = R // 2
+FIRST_POS = 384
+TWO_PI = 6.283185307179586
+
+FLOPS = 2 * T * B * 3 * M * M
+
+F32 = mybir.dt.float32
+BF16 = mybir.dt.bfloat16
+I32 = mybir.dt.int32
+U32 = mybir.dt.uint32
+U8 = mybir.dt.uint8
+FP8 = mybir.dt.float8_e4m3fn
+FP8X4 = mybir.dt.float8_e4m3fn_x4
+ALU = mybir.AluOpType
+ACT = mybir.ActivationFunctionType
+
+LOAD_AHEAD = 8
+V_PAIRS = [16, 17, 18, 19] + list(range(16))
+S_GROUPS = [[40, 41, 42, 43], [44, 45, 46, 47]]
+GS = 4
+BG_STEPS = 36
+V_INTERLEAVES = (1, 6)
+
+
+def tile_multiheadattention_pa_kernel(tc, x, w_bytes, w_scale, bias, out_0, out_1, out_2):
+    nc = tc.nc
+    outs = (out_0, out_1, out_2)
+    v_heads = [2 * pr + a for pr in V_PAIRS for a in range(2)]
+    NV = len(v_heads)
+
+    with ExitStack() as ctx:
+        const = ctx.enter_context(tc.tile_pool(name="const", bufs=1))
+        bytes_pool = ctx.enter_context(tc.tile_pool(name="bytes_pool", bufs=LOAD_AHEAD + 2))
+        sbytes_pool = ctx.enter_context(tc.tile_pool(name="sbytes_pool", bufs=2 * GS))
+        work = ctx.enter_context(tc.tile_pool(name="work", bufs=3))
+        spath = ctx.enter_context(tc.tile_pool(name="spath", bufs=2))
+        tp_pool = ctx.enter_context(tc.psum_pool(name="tp_pool", bufs=4))
+        acc_pool = ctx.enter_context(tc.psum_pool(name="acc_pool", bufs=2))
+        yt_pool = ctx.enter_context(tc.psum_pool(name="yt_pool", bufs=2))
+
+        zero = const.tile([P, 1], F32, name="zero")
+        nc.vector.memset(zero[:], 0.0)
+        warm = const.tile([P, 1], F32, name="warm")
+        nc.scalar.activation(out=warm[:], in_=zero[:], func=ACT.Sin)
+
+        pos_f = const.tile([P, 1], F32, name="pos_f")
+        nc.gpsimd.iota(out=pos_f[:], pattern=[[0, 1]], base=FIRST_POS, channel_multiplier=1,
+                       allow_small_or_imprecise_dtypes=True)
+        ident = const.tile([P, P], F32, name="ident")
+        make_identity(nc, ident[:])
+        ident_bf = const.tile([P, P], BF16, name="ident_bf")
+        make_identity(nc, ident_bf[:])
+        braw = const.tile([P, P], BF16, name="braw")
+        nc.gpsimd.memset(braw[:], 0.0)
+        swap = const.tile([P, NP * 2, 2], F32, name="swap")
+        nc.gpsimd.tensor_copy(out=swap[:], in_=ident[:].rearrange("p (i e) -> p i e", e=2)[:, :, ::-1])
+        turns = const.tile([P, NP], F32, name="turns")
+        nc.vector.tensor_scalar(out=turns[:, 0:1], in0=pos_f[:], scalar1=1.0 / TWO_PI, scalar2=None, op0=ALU.mult)
+        for w in (1, 2, 4, 8, 16):
+            nc.vector.tensor_scalar(out=turns[:, w:2 * w], in0=turns[:, 0:w], scalar1=10000.0 ** (-2.0 * w / R),
+                                    scalar2=None, op0=ALU.mult)
+
+        s_flat = w_scale.rearrange("o k -> (o k)")
+        s_bc = const.tile([P, M], F32, name="s_bc")
+        wbyte, sbyte = {}, {}
+
+        def load_scale(c):
+            nc.sync.dma_start(out=s_bc[:, c * 512:(c + 1) * 512],
+                              in_=s_flat[c * 512:(c + 1) * 512].partition_broadcast(P))
+
+        def load(h):
+            wbyte[h] = bytes_pool.tile([P, M], U8, name="wbyte")
+            nc.sync.dma_start(out=wbyte[h][:], in_=w_bytes[h * P:(h + 1) * P, :])
+
+        def load_s(h):
+            sbyte[h] = sbytes_pool.tile([P, M], U8, name="sbyte")
+            nc.sync.dma_start(out=sbyte[h][:], in_=w_bytes[h * P:(h + 1) * P, :])
+
+        xs = const.tile([P, B, M], BF16, name="xs")
+        load_scale(0)
+        load(v_heads[0])
+        load_s(S_GROUPS[0][0])
+        for c in range(1, 4):
+            load_scale(c)
+        load_s(S_GROUPS[0][1])
+        load(v_heads[1])
+        load_s(S_GROUPS[0][2])
+        for b in range(B):
+            nc.sync.dma_start(out=xs[:, b, :], in_=x[:, b, :])
+        load(v_heads[2])
+        load_s(S_GROUPS[0][3])
+        for s in range(3, LOAD_AHEAD):
+            load(v_heads[s])
+        for h in S_GROUPS[1]:
+            load_s(h)
+        qk_bias = bias[0:2 * M].rearrange("(q a k c) -> k q a c", a=2, k=2, c=R)
+        for kind in range(2):
+            nc.scalar.dma_start(out=braw[kind * H:(kind + 1) * H, :].rearrange("q (a c) -> q a c", a=2),
+                                in_=qk_bias[kind])
+        nc.scalar.dma_start(out=braw[2 * H:NH, :], in_=bias[2 * M:3 * M].rearrange("(c p) -> c p", p=P))
+        s_col = const.tile([P, G, 4], F32, name="s_col")
+        nc.scalar.dma_start(out=s_col[:], in_=w_scale.rearrange("o (g p t) -> p (o g) t", g=G, p=P, t=4))
+
+        trig_tab = const.tile([P, 2, B, T], F32, name="trig_tab")
+
+        def tables_vector():
+            whole_i = const.tile([P, NP], I32, name="whole_i")
+            nc.vector.tensor_copy(out=whole_i[:], in_=turns[:])
+            whole_f = const.tile([P, NP], F32, name="whole_f")
+            nc.vector.tensor_copy(out=whole_f[:], in_=whole_i[:])
+            frac_s = const.tile([P, NP], F32, name="frac_s")
+            nc.vector.tensor_tensor(out=frac_s[:], in0=turns[:], in1=whole_f[:], op=ALU.subtract)
+            frac_c = const.tile([P, NP], F32, name="frac_c")
+            nc.vector.tensor_scalar(out=frac_c[:], in0=frac_s[:], scalar1=0.25, scalar2=None, op0=ALU.add)
+            neg = {}
+            for name, frac in (("s", frac_s), ("c", frac_c)):
+                neg[name] = const.tile([P, NP], F32, name="neg_" + name)
+                nc.vector.scalar_tensor_tensor(out=neg[name][:], in0=frac[:], scalar=0.5, in1=frac[:],
+                                               op0=ALU.is_ge, op1=ALU.subtract)
+            return neg
+
+        def tables_rest(neg):
+            cos_f = const.tile([P, 2, NP, 2], F32, name="cos_f")
+            sin_f = const.tile([P, 2, NP, 2], F32, name="sin_f")
+            nc.scalar.activation(out=cos_f[:], in_=neg["c"][:].unsqueeze(1).unsqueeze(3).to_broadcast([P, 2, NP, 2]),
+                                 func=ACT.Sin, scale=-TWO_PI)
+            for e in range(2):
+                nc.scalar.activation(out=sin_f[:, :, :, e], in_=neg["s"][:].unsqueeze(1).to_broadcast([P, 2, NP]),
+                                     func=ACT.Sin, scale=(-TWO_PI if e == 0 else TWO_PI))
+            tab_ps = tp_pool.tile([P, 2, 2, P], F32, name="tp")
+            nc.tensor.transpose(tab_ps[:, 0, 0, :], cos_f[:].rearrange("p a i e -> p (a i e)"), ident[:])
+            nc.tensor.transpose(tab_ps[:, 0, 1, :], sin_f[:].rearrange("p a i e -> p (a i e)"), ident[:])
+            for b in range(B):
+                nc.scalar.copy(out=trig_tab[:, :, b, :], in_=tab_ps[:, 0, :, :])
+
+        neg_turns = tables_vector()
+
+        wb, grp, y, bm, yt, ot = {}, {}, {}, {}, {}, {}
+        lhs = {}
+
+        def widen(h, pieces):
+            wb[h] = work.tile([P, M], BF16, name="wb")
+            w = M // pieces
+            for c in range(pieces):
+                nc.vector.tensor_tensor(out=wb[h][:, c * w:(c + 1) * w],
+                                        in0=wbyte[h][:, c * w:(c + 1) * w].bitcast(FP8),
+                                        in1=s_bc[:, c * w:(c + 1) * w], op=ALU.mult)
+
+        def turn_words(words, dst_of_half, split_rows):
+            for half in range(2):
+                tp = tp_pool.tile([P, 2, 2, P], F32, name="tp")
+                for gg in range(2):
+                    g = 2 * half + gg
+                    for u in range(2):
+                        nc.tensor.transpose(tp[:, u, gg, :], words[:, 256 * g + u:256 * (g + 1):2], ident[:])
+                if split_rows:
+                    src = tp[:].rearrange("p u g (k r) -> p (g k) r u", k=2)
+                else:
+                    src = tp[:].rearrange("p u g r -> p g r u")
+                nc.scalar.copy(out=dst_of_half(half), in_=src)
+
+        def turn(h):
+            pair, a = h // 2, h % 2
+            if a == 0:
+                grp[pair] = work.tile([P, G, 2, P, 2], F32, name="grp", align_bytes=64)
+            if pair < H:
+                blocks = grp[pair][:].rearrange("p g k c u -> p (g k) c u")
+                turn_words(wb[h][:].bitcast(F32),
+                           lambda half: blocks[:, 4 * half:4 * half + 4, a * R:(a + 1) * R, :], True)
+            else:
+                turn_words(wb[h][:].bitcast(F32),
+                           lambda half: grp[pair][:, 2 * half:2 * half + 2, a, :, :], False)
+
+        def quantize(pair):
+            codes = work.tile([P, 2 * G * P], U32, name="codes", align_bytes=64)
+            sc = work.tile([P, 2 * G * P], U8, name="sc", align_bytes=64)
+            nc.vector.quantize_mx(out=codes[:].bitcast(FP8X4), scales=sc[:],
+                                  in_=grp[pair][:].rearrange("p g k c u -> p (g k c u)").bitcast(BF16))
+            for kind in range(2):
+                lhs[(pair, kind)] = [(codes[:, (2 * g + kind) * P:(2 * g + kind + 1) * P],
+                                      sc[:, (2 * g + kind) * P:(2 * g + kind + 1) * P]) for g in range(G)]
+
+        gx = const.tile([P, G, B * T, 2], F32, name="gx", align_bytes=64)
+        x_codes = const.tile([P, G * B * T], U32, name="x_codes", align_bytes=64)
+        x_sc = const.tile([P, G * B * T], U8, name="x_sc", align_bytes=64)
+        bias_col = const.tile([P, NH], F32, name="bias_col")
+
+        def prepare_x():
+            for b in range(B):
+                turn_words(xs[:, b, :].bitcast(F32),
+                           lambda half: gx[:, 2 * half:2 * half + 2, b * T:(b + 1) * T, :], False)
+
+        def prepare_bias():
+            braw32 = const.tile([P, P], F32, name="braw32")
+            nc.scalar.copy(out=braw32[:], in_=braw[:])
+            bias_ps = tp_pool.tile([P, 2, 2, P], F32, name="tp")
+            nc.tensor.transpose(bias_ps[:, 0, 0, :], braw32[:], ident[:])
+            nc.scalar.copy(out=bias_col[:], in_=bias_ps[:, 0, 0, 0:NH])
+
+        def quantize_x():
+            nc.vector.quantize_mx(out=x_codes[:].bitcast(FP8X4), scales=x_sc[:],
+                                  in_=gx[:].rearrange("p g r u -> p (g r u)").bitcast(BF16))
+
+        def bias_of(pair, kind):
+            col = kind * H + pair if pair < H else 2 * pair + kind
+            return bias_col[:, col:col + 1]
+
+        def multiply(pair, kind):
+            tile_acc = acc_pool.tile([P, B * T], F32, name="acc")
+            if kind == 0:
+                y[pair] = work.tile([P, 2, B * T], F32, name="y")
+            for g in range(G):
+                nc.tensor.matmul_mx(out=tile_acc[:],
+                                    lhsT=lhs[(pair, kind)][g][0].bitcast(FP8X4),
+                                    lhsT_scale=lhs[(pair, kind)][g][1],
+                                    rhs=x_codes[:, g * B * T:(g + 1) * B * T].bitcast(FP8X4),
+                                    rhs_scale=x_sc[:, g * B * T:(g + 1) * B * T],
+                                    start=(g == 0), stop=(g == G - 1))
+            if pair < H and kind == 0:
+                bm[pair] = work.tile([P, 2, B, T], F32, name="bm")
+                nc.vector.scalar_tensor_tensor(
+                    out=bm[pair][:].rearrange("p j b t -> p j (b t)"),
+                    in0=tile_acc[:].unsqueeze(1).to_broadcast([P, 2, B * T]),
+                    scalar=bias_of(pair, 0),
+                    in1=trig_tab[:].rearrange("p j b t -> p j (b t)"),
+                    op0=ALU.add, op1=ALU.mult)
+            else:
+                nc.scalar.activation(out=y[pair][:, kind, :], in_=tile_acc[:], func=ACT.Identity,
+                                     bias=bias_of(pair, kind), scale=1.0)
+
+        def turn_back(pair):
+            yt[pair] = yt_pool.tile([P, 2, B, DH], F32, name="yt")
+            for kind in range(2):
+                for b in range(B):
+                    if pair < H and kind == 0:
+                        nc.tensor.matmul(out=yt[pair][:, 0, b, :], lhsT=bm[pair][:, 0, b, :],
+                                         rhs=ident[:], is_transpose=True, start=True, stop=False)
+                        nc.tensor.matmul(out=yt[pair][:, 0, b, :], lhsT=bm[pair][:, 1, b, :],
+                                         rhs=swap[:].rearrange("p i e -> p (i e)"), is_transpose=True,
+                                         start=False, stop=True)
+                    else:
+                        nc.tensor.transpose(yt[pair][:, kind, b, :], y[pair][:, kind, b * T:(b + 1) * T], ident[:])
+            ot[pair] = work.tile([P, B, 2, DH], F32, name="ot", bufs=4)
+            if pair < H:
+                nc.scalar.copy(out=ot[pair][:].rearrange("p b a (k c) -> p k (b a) c", k=2),
+                               in_=yt[pair][:].rearrange("p k b (a c) -> p k (b a) c", a=2))
+            else:
+                nc.scalar.copy(out=ot[pair][:].rearrange("p b a c -> p a b c"), in_=yt[pair][:])
+            j, h0 = pair // (H // 2), 2 * (pair % (H // 2))
+            nc.sync.dma_start(out=outs[j][:, :, h0:h0 + 2, :], in_=ot[pair][:])
+
+        wbs, planes, grps = {}, {}, {}
+
+        def s_widen(k, j):
+            h = S_GROUPS[k][j]
+            wbs[h] = spath.tile([P, M], BF16, name="wbs", bufs=GS)
+            nc.scalar.copy(out=wbs[h][:], in_=sbyte[h][:].bitcast(FP8))
+
+        def s_planes(k, g, t0):
+            if t0 == 0:
+                planes[(k, g)] = spath.tile([P, 4, GS * P], BF16, name="planes")
+            for t in (t0, t0 + 1):
+                tpb = tp_pool.tile([P, GS, P], BF16, name="tp")
+                for j in range(GS):
+                    nc.tensor.transpose(tpb[:, j, :], wbs[S_GROUPS[k][j]][:, 512 * g + t:512 * (g + 1):4], ident_bf[:])
+                nc.scalar.activation(out=planes[(k, g)][:, t, :], in_=tpb[:].rearrange("p j r -> p (j r)"),
+                                     func=ACT.Copy, scale=s_col[:, g, t:t + 1])
+
+        def s_interleave(k, g):
+            grps[(k, g)] = spath.tile([P, GS * P, 4], BF16, name="grps", align_bytes=64)
+            if G * k + g in V_INTERLEAVES:
+                nc.vector.tensor_copy(out=grps[(k, g)][:], in_=planes[(k, g)][:].rearrange("p t c -> p c t"))
+            else:
+                nc.scalar.copy(out=grps[(k, g)][:].rearrange("p (c i) t -> p c t i", i=4),
+                               in_=planes[(k, g)][:].rearrange("p t (c i) -> p c t i", i=4))
+
+        def s_quantize(k, g):
+            codes = spath.tile([P, GS * P], U32, name="codes_s", bufs=2 * G, align_bytes=64)
+            sc = spath.tile([P, GS * P], U8, name="sc_s", bufs=2 * G, align_bytes=64)
+            nc.vector.quantize_mx(out=codes[:].bitcast(FP8X4), scales=sc[:],
+                                  in_=grps[(k, g)][:].rearrange("p c t -> p (c t)"))
+            for j in range(GS):
+                h = S_GROUPS[k][j]
+                lhs.setdefault((h // 2, h % 2), []).append((codes[:, j * P:(j + 1) * P], sc[:, j * P:(j + 1) * P]))
+
+        background = []
+        for k in range(len(S_GROUPS)):
+            for j in range(GS):
+                background.append(("widen", k, j))
+            for g in range(G):
+                background.append(("planes", k, g, 0))
+                background.append(("planes", k, g, 2))
+                background.append(("interleave", k, g))
+        bg_at, quant_at, mult_at, back_at, squant_at = {}, {}, {}, {}, {}
+        for s in range(1, NV, 2):
+            quant_at[s + 2] = v_heads[s] // 2
+            mult_at.setdefault(s + 3, []).append((v_heads[s] // 2, 0))
+            mult_at.setdefault(s + 4, []).append((v_heads[s] // 2, 1))
+            back_at.setdefault(s + 5, []).append(v_heads[s] // 2)
+        for n in range(len(background)):
+            task = background[n]
+            s = (n * BG_STEPS) // len(background)
+            bg_at.setdefault(s, []).append(task)
+            if task[0] == "interleave":
+                squant_at.setdefault(s + 1, []).append((task[1], task[2]))
+                if task[2] == G - 1:
+                    for j in range(GS):
+                        mult_at.setdefault(s + 2 + j, []).append((S_GROUPS[task[1]][j] // 2, j % 2))
+                        if j % 2 == 1:
+                            back_at.setdefault(s + 3 + j, []).append(S_GROUPS[task[1]][j] // 2)
+        last_step = max(back_at)
+
+        for s in range(last_step + 1):
+            if s + LOAD_AHEAD < NV:
+                load(v_heads[s + LOAD_AHEAD])
+            if 0 <= s - 1 < NV:
+                turn(v_heads[s - 1])
+            if s == 0:
+                prepare_x()
+            if s == 1:
+                prepare_bias()
+            if s < NV:
+                widen(v_heads[s], 4 if s == 0 else 1)
+            if s == 4:
+                tables_rest(neg_turns)
+            for pk in mult_at.get(s, []):
+                multiply(pk[0], pk[1])
+            for pair in back_at.get(s, []):
+                turn_back(pair)
+            if s == 2:
+                quantize_x()
+            if s in quant_at:
+                quantize(quant_at[s])
+            for task in bg_at.get(s, []):
+                if task[0] == "widen":
+                    s_widen(task[1], task[2])
+                elif task[0] == "planes":
+                    s_planes(task[1], task[2], task[3])
+                else:
+                    s_interleave(task[1], task[2])
+            for kg in squant_at.get(s, []):
+                s_quantize(kg[0], kg[1])

@@ -29,7 +29,7 @@ V_PAIRS = [16, 17, 18, 19] + list(range(16))
 S_GROUPS = [[40, 41, 42, 43], [44, 45, 46, 47]]
 GS = 4
 BG_STEPS = 36
-V_INTERLEAVES = (1, 6)
+V_INTERLEAVES = ()
 
 
 def tile_multiheadattention_pa_kernel(tc, x, w_bytes, w_scale, bias, out_0, out_1, out_2):

@@ -48,6 +48,9 @@ def tile_multiheadattention_pa_kernel(tc, x, w_bytes, w_scale, bias, out_0, out_
         acc_pool = ctx.enter_context(tc.psum_pool(name="acc_pool", bufs=2))
         yt_pool = ctx.enter_context(tc.psum_pool(name="yt_pool", bufs=2))
 
+        s_col = const.tile([P, G, 4], F32, name="s_col")
+        nc.scalar.dma_start(out=s_col[:], in_=w_scale.rearrange("o (g p t) -> p (o g) t", g=G, p=P, t=4))
+
         zero = const.tile([P, 1], F32, name="zero")
         nc.vector.memset(zero[:], 0.0)
         warm = const.tile([P, 1], F32, name="warm")
@@ -70,13 +73,8 @@ def tile_multiheadattention_pa_kernel(tc, x, w_bytes, w_scale, bias, out_0, out_
             nc.vector.tensor_scalar(out=turns[:, w:2 * w], in0=turns[:, 0:w], scalar1=10000.0 ** (-2.0 * w / R),
                                     scalar2=None, op0=ALU.mult)
 
-        s_flat = w_scale.rearrange("o k -> (o k)")
         s_bc = const.tile([P, M], F32, name="s_bc")
         wbyte, sbyte = {}, {}
-
-        def load_scale(c):
-            nc.sync.dma_start(out=s_bc[:, c * 512:(c + 1) * 512],
-                              in_=s_flat[c * 512:(c + 1) * 512].partition_broadcast(P))
 
         def load(h):
             wbyte[h] = bytes_pool.tile([P, M], U8, name="wbyte")
@@ -87,11 +85,8 @@ def tile_multiheadattention_pa_kernel(tc, x, w_bytes, w_scale, bias, out_0, out_
             nc.sync.dma_start(out=sbyte[h][:], in_=w_bytes[h * P:(h + 1) * P, :])
 
         xs = const.tile([P, B, M], BF16, name="xs")
-        load_scale(0)
         load(v_heads[0])
         load_s(S_GROUPS[0][0])
-        for c in range(1, 4):
-            load_scale(c)
         load_s(S_GROUPS[0][1])
         load(v_heads[1])
         load_s(S_GROUPS[0][2])
@@ -108,8 +103,17 @@ def tile_multiheadattention_pa_kernel(tc, x, w_bytes, w_scale, bias, out_0, out_
             nc.scalar.dma_start(out=braw[kind * H:(kind + 1) * H, :].rearrange("q (a c) -> q a c", a=2),
                                 in_=qk_bias[kind])
         nc.scalar.dma_start(out=braw[2 * H:NH, :], in_=bias[2 * M:3 * M].rearrange("(c p) -> c p", p=P))
-        s_col = const.tile([P, G, 4], F32, name="s_col")
-        nc.scalar.dma_start(out=s_col[:], in_=w_scale.rearrange("o (g p t) -> p (o g) t", g=G, p=P, t=4))
+
+        for g in range(G):
+            sp = tp_pool.tile([P, 2, 2, P], F32, name="tp")
+            sp4 = sp[:].rearrange("p a b n -> p (a b) n")
+            for t in range(4):
+                nc.tensor.transpose(sp4[:, t, :], s_col[:, g, t:t + 1].to_broadcast([P, P]), ident[:])
+            spread_dst = s_bc[:, g * 512:(g + 1) * 512].rearrange("p (n t) -> p n t", t=4)
+            if g < 2:
+                nc.vector.tensor_copy(out=spread_dst, in_=sp4.rearrange("p t n -> p n t"))
+            else:
+                nc.scalar.copy(out=spread_dst, in_=sp4.rearrange("p t n -> p n t"))
 
         trig_tab = const.tile([P, 2, B, T], F32, name="trig_tab")
 

@@ -110,7 +110,7 @@ def tile_multiheadattention_pa_kernel(tc, x, w_bytes, w_scale, bias, out_0, out_
             for t in range(4):
                 nc.tensor.transpose(sp4[:, t, :], s_col[:, g, t:t + 1].to_broadcast([P, P]), ident[:])
             spread_dst = s_bc[:, g * 512:(g + 1) * 512].rearrange("p (n t) -> p n t", t=4)
-            if g < 2:
+            if g < 4:
                 nc.vector.tensor_copy(out=spread_dst, in_=sp4.rearrange("p t n -> p n t"))
             else:
                 nc.scalar.copy(out=spread_dst, in_=sp4.rearrange("p t n -> p n t"))

@@ -273,12 +273,15 @@ def tile_multiheadattention_pa_kernel(tc, x, w_bytes, w_scale, bias, out_0, out_
         def s_planes(k, g, t0):
             if t0 == 0:
                 planes[(k, g)] = spath.tile([P, 4, GS * P], BF16, name="planes")
-            for t in (t0, t0 + 1):
-                tpb = tp_pool.tile([P, GS, P], BF16, name="tp")
-                for j in range(GS):
-                    nc.tensor.transpose(tpb[:, j, :], wbs[S_GROUPS[k][j]][:, 512 * g + t:512 * (g + 1):4], ident_bf[:])
-                nc.scalar.activation(out=planes[(k, g)][:, t, :], in_=tpb[:].rearrange("p j r -> p (j r)"),
-                                     func=ACT.Copy, scale=s_col[:, g, t:t + 1])
+            u = t0 // 2
+            tpw = tp_pool.tile([P, GS, P], F32, name="tp")
+            for j in range(GS):
+                nc.tensor.transpose(tpw[:, j, :], wbs[S_GROUPS[k][j]][:].bitcast(F32)[:, 256 * g + u:256 * (g + 1):2],
+                                    ident[:])
+            both = tpw[:].rearrange("p j r -> p (j r)").bitcast(BF16).rearrange("p (c e) -> p c e", e=2)
+            for e in range(2):
+                nc.scalar.activation(out=planes[(k, g)][:, t0 + e, :], in_=both[:, :, e],
+                                     func=ACT.Copy, scale=s_col[:, g, t0 + e:t0 + e + 1])
 
         def s_interleave(k, g):
             grps[(k, g)] = spath.tile([P, GS * P, 4], BF16, name="grps", align_bytes=64)

from contextlib import ExitStack

import concourse.mybir as mybir
from concourse.masks import make_identity

T, B, H, DH, R = 128, 2, 16, 128, 64
M = H * DH
NH = 3 * H
P = 128
G = 4
NP = R // 2
FIRST_POS = 384
TWO_PI = 6.283185307179586

FLOPS = 2 * T * B * 3 * M * M

F32 = mybir.dt.float32
BF16 = mybir.dt.bfloat16
I32 = mybir.dt.int32
U32 = mybir.dt.uint32
U8 = mybir.dt.uint8
FP8 = mybir.dt.float8_e4m3fn
FP8X4 = mybir.dt.float8_e4m3fn_x4
ALU = mybir.AluOpType
ACT = mybir.ActivationFunctionType

LOAD_AHEAD = 8
V_PAIRS = [16, 17, 18, 19] + list(range(16))
S_GROUPS = [[40, 41, 42, 43], [44, 45, 46, 47]]
GS = 4
BG_STEPS = 36
V_INTERLEAVES = ()


def tile_multiheadattention_pa_kernel(tc, x, w_bytes, w_scale, bias, out_0, out_1, out_2):
    nc = tc.nc
    outs = (out_0, out_1, out_2)
    v_heads = [2 * pr + a for pr in V_PAIRS for a in range(2)]
    NV = len(v_heads)

    with ExitStack() as ctx:
        const = ctx.enter_context(tc.tile_pool(name="const", bufs=1))
        bytes_pool = ctx.enter_context(tc.tile_pool(name="bytes_pool", bufs=LOAD_AHEAD + 2))
        sbytes_pool = ctx.enter_context(tc.tile_pool(name="sbytes_pool", bufs=2 * GS))
        work = ctx.enter_context(tc.tile_pool(name="work", bufs=3))
        spath = ctx.enter_context(tc.tile_pool(name="spath", bufs=2))
        tp_pool = ctx.enter_context(tc.psum_pool(name="tp_pool", bufs=4))
        acc_pool = ctx.enter_context(tc.psum_pool(name="acc_pool", bufs=2))
        yt_pool = ctx.enter_context(tc.psum_pool(name="yt_pool", bufs=2))

        s_col = const.tile([P, G, 4], F32, name="s_col")
        nc.scalar.dma_start(out=s_col[:], in_=w_scale.rearrange("o (g p t) -> p (o g) t", g=G, p=P, t=4))

        zero = const.tile([P, 1], F32, name="zero")
        nc.vector.memset(zero[:], 0.0)
        warm = const.tile([P, 1], F32, name="warm")
        nc.scalar.activation(out=warm[:], in_=zero[:], func=ACT.Sin)

        pos_f = const.tile([P, 1], F32, name="pos_f")
        nc.gpsimd.iota(out=pos_f[:], pattern=[[0, 1]], base=FIRST_POS, channel_multiplier=1,
                       allow_small_or_imprecise_dtypes=True)
        ident = const.tile([P, P], F32, name="ident")
        make_identity(nc, ident[:])
        ident_bf = const.tile([P, P], BF16, name="ident_bf")
        make_identity(nc, ident_bf[:])
        braw = const.tile([P, P], BF16, name="braw")
        nc.gpsimd.memset(braw[:], 0.0)
        swap = const.tile([P, NP * 2, 2], F32, name="swap")
        nc.gpsimd.tensor_copy(out=swap[:], in_=ident[:].rearrange("p (i e) -> p i e", e=2)[:, :, ::-1])
        turns = const.tile([P, NP], F32, name="turns")
        nc.vector.tensor_scalar(out=turns[:, 0:1], in0=pos_f[:], scalar1=1.0 / TWO_PI, scalar2=None, op0=ALU.mult)
        for w in (1, 2, 4, 8, 16):
            nc.vector.tensor_scalar(out=turns[:, w:2 * w], in0=turns[:, 0:w], scalar1=10000.0 ** (-2.0 * w / R),
                                    scalar2=None, op0=ALU.mult)

        s_bc = const.tile([P, M], F32, name="s_bc")
        wbyte, sbyte = {}, {}

        def load(h):
            wbyte[h] = bytes_pool.tile([P, M], U8, name="wbyte")
            nc.sync.dma_start(out=wbyte[h][:], in_=w_bytes[h * P:(h + 1) * P, :])

        def load_s(h):
            sbyte[h] = sbytes_pool.tile([P, M], U8, name="sbyte")
            nc.sync.dma_start(out=sbyte[h][:], in_=w_bytes[h * P:(h + 1) * P, :])

        xs = const.tile([P, B, M], BF16, name="xs")
        load(v_heads[0])
        load_s(S_GROUPS[0][0])
        load_s(S_GROUPS[0][1])
        load(v_heads[1])
        load_s(S_GROUPS[0][2])
        for b in range(B):
            nc.sync.dma_start(out=xs[:, b, :], in_=x[:, b, :])
        load(v_heads[2])
        load_s(S_GROUPS[0][3])
        for s in range(3, LOAD_AHEAD):
            load(v_heads[s])
        for h in S_GROUPS[1]:
            load_s(h)
        qk_bias = bias[0:2 * M].rearrange("(q a k c) -> k q a c", a=2, k=2, c=R)
        for kind in range(2):
            nc.scalar.dma_start(out=braw[kind * H:(kind + 1) * H, :].rearrange("q (a c) -> q a c", a=2),
                                in_=qk_bias[kind])
        nc.scalar.dma_start(out=braw[2 * H:NH, :], in_=bias[2 * M:3 * M].rearrange("(c p) -> c p", p=P))

        for g in range(G):
            sp = tp_pool.tile([P, 2, 2, P], F32, name="tp")
            sp4 = sp[:].rearrange("p a b n -> p (a b) n")
            for t in range(4):
                nc.tensor.transpose(sp4[:, t, :], s_col[:, g, t:t + 1].to_broadcast([P, P]), ident[:])
            spread_dst = s_bc[:, g * 512:(g + 1) * 512].rearrange("p (n t) -> p n t", t=4)
            if g < 4:
                nc.vector.tensor_copy(out=spread_dst, in_=sp4.rearrange("p t n -> p n t"))
            else:
                nc.scalar.copy(out=spread_dst, in_=sp4.rearrange("p t n -> p n t"))

        trig_tab = const.tile([P, 2, B, T], F32, name="trig_tab")

        def tables_vector():
            whole_i = const.tile([P, NP], I32, name="whole_i")
            nc.vector.tensor_copy(out=whole_i[:], in_=turns[:])
            whole_f = const.tile([P, NP], F32, name="whole_f")
            nc.vector.tensor_copy(out=whole_f[:], in_=whole_i[:])
            frac_s = const.tile([P, NP], F32, name="frac_s")
            nc.vector.tensor_tensor(out=frac_s[:], in0=turns[:], in1=whole_f[:], op=ALU.subtract)
            frac_c = const.tile([P, NP], F32, name="frac_c")
            nc.vector.tensor_scalar(out=frac_c[:], in0=frac_s[:], scalar1=0.25, scalar2=None, op0=ALU.add)
            neg = {}
            for name, frac in (("s", frac_s), ("c", frac_c)):
                neg[name] = const.tile([P, NP], F32, name="neg_" + name)
                nc.vector.scalar_tensor_tensor(out=neg[name][:], in0=frac[:], scalar=0.5, in1=frac[:],
                                               op0=ALU.is_ge, op1=ALU.subtract)
            return neg

        def tables_rest(neg):
            cos_f = const.tile([P, 2, NP, 2], F32, name="cos_f")
            sin_f = const.tile([P, 2, NP, 2], F32, name="sin_f")
            nc.scalar.activation(out=cos_f[:], in_=neg["c"][:].unsqueeze(1).unsqueeze(3).to_broadcast([P, 2, NP, 2]),
                                 func=ACT.Sin, scale=-TWO_PI)
            for e in range(2):
                nc.scalar.activation(out=sin_f[:, :, :, e], in_=neg["s"][:].unsqueeze(1).to_broadcast([P, 2, NP]),
                                     func=ACT.Sin, scale=(-TWO_PI if e == 0 else TWO_PI))
            tab_ps = tp_pool.tile([P, 2, 2, P], F32, name="tp")
            nc.tensor.transpose(tab_ps[:, 0, 0, :], cos_f[:].rearrange("p a i e -> p (a i e)"), ident[:])
            nc.tensor.transpose(tab_ps[:, 0, 1, :], sin_f[:].rearrange("p a i e -> p (a i e)"), ident[:])
            for b in range(B):
                nc.scalar.copy(out=trig_tab[:, :, b, :], in_=tab_ps[:, 0, :, :])

        neg_turns = tables_vector()

        wb, grp, y, bm, yt, ot = {}, {}, {}, {}, {}, {}
        lhs = {}

        def widen(h, pieces):
            wb[h] = work.tile([P, M], BF16, name="wb")
            w = M // pieces
            for c in range(pieces):
                nc.vector.tensor_tensor(out=wb[h][:, c * w:(c + 1) * w],
                                        in0=wbyte[h][:, c * w:(c + 1) * w].bitcast(FP8),
                                        in1=s_bc[:, c * w:(c + 1) * w], op=ALU.mult)

        def turn_words(words, dst_of_half, split_rows):
            for half in range(2):
                tp = tp_pool.tile([P, 2, 2, P], F32, name="tp")
                for gg in range(2):
                    g = 2 * half + gg
                    for u in range(2):
                        nc.tensor.transpose(tp[:, u, gg, :], words[:, 256 * g + u:256 * (g + 1):2], ident[:])
                if split_rows:
                    src = tp[:].rearrange("p u g (k r) -> p (g k) r u", k=2)
                else:
                    src = tp[:].rearrange("p u g r -> p g r u")
                nc.scalar.copy(out=dst_of_half(half), in_=src)

        def turn(h):
            pair, a = h // 2, h % 2
            if a == 0:
                grp[pair] = work.tile([P, G, 2, P, 2], F32, name="grp", align_bytes=64)
            if pair < H:
                blocks = grp[pair][:].rearrange("p g k c u -> p (g k) c u")
                turn_words(wb[h][:].bitcast(F32),
                           lambda half: blocks[:, 4 * half:4 * half + 4, a * R:(a + 1) * R, :], True)
            else:
                turn_words(wb[h][:].bitcast(F32),
                           lambda half: grp[pair][:, 2 * half:2 * half + 2, a, :, :], False)

        def quantize(pair):
            codes = work.tile([P, 2 * G * P], U32, name="codes", align_bytes=64)
            sc = work.tile([P, 2 * G * P], U8, name="sc", align_bytes=64)
            nc.vector.quantize_mx(out=codes[:].bitcast(FP8X4), scales=sc[:],
                                  in_=grp[pair][:].rearrange("p g k c u -> p (g k c u)").bitcast(BF16))
            for kind in range(2):
                lhs[(pair, kind)] = [(codes[:, (2 * g + kind) * P:(2 * g + kind + 1) * P],
                                      sc[:, (2 * g + kind) * P:(2 * g + kind + 1) * P]) for g in range(G)]

        gx = const.tile([P, G, B * T, 2], F32, name="gx", align_bytes=64)
        x_codes = const.tile([P, G * B * T], U32, name="x_codes", align_bytes=64)
        x_sc = const.tile([P, G * B * T], U8, name="x_sc", align_bytes=64)
        bias_col = const.tile([P, NH], F32, name="bias_col")

        def prepare_x():
            for b in range(B):
                turn_words(xs[:, b, :].bitcast(F32),
                           lambda half: gx[:, 2 * half:2 * half + 2, b * T:(b + 1) * T, :], False)

        def prepare_bias():
            braw32 = const.tile([P, P], F32, name="braw32")
            nc.scalar.copy(out=braw32[:], in_=braw[:])
            bias_ps = tp_pool.tile([P, 2, 2, P], F32, name="tp")
            nc.tensor.transpose(bias_ps[:, 0, 0, :], braw32[:], ident[:])
            nc.scalar.copy(out=bias_col[:], in_=bias_ps[:, 0, 0, 0:NH])

        def quantize_x():
            nc.vector.quantize_mx(out=x_codes[:].bitcast(FP8X4), scales=x_sc[:],
                                  in_=gx[:].rearrange("p g r u -> p (g r u)").bitcast(BF16))

        def bias_of(pair, kind):
            col = kind * H + pair if pair < H else 2 * pair + kind
            return bias_col[:, col:col + 1]

        def multiply(pair, kind):
            tile_acc = acc_pool.tile([P, B * T], F32, name="acc")
            if kind == 0:
                y[pair] = work.tile([P, 2, B * T], F32, name="y")
            for g in range(G):
                nc.tensor.matmul_mx(out=tile_acc[:],
                                    lhsT=lhs[(pair, kind)][g][0].bitcast(FP8X4),
                                    lhsT_scale=lhs[(pair, kind)][g][1],
                                    rhs=x_codes[:, g * B * T:(g + 1) * B * T].bitcast(FP8X4),
                                    rhs_scale=x_sc[:, g * B * T:(g + 1) * B * T],
                                    start=(g == 0), stop=(g == G - 1))
            if pair < H and kind == 0:
                bm[pair] = work.tile([P, 2, B, T], F32, name="bm")
                nc.vector.scalar_tensor_tensor(
                    out=bm[pair][:].rearrange("p j b t -> p j (b t)"),
                    in0=tile_acc[:].unsqueeze(1).to_broadcast([P, 2, B * T]),
                    scalar=bias_of(pair, 0),
                    in1=trig_tab[:].rearrange("p j b t -> p j (b t)"),
                    op0=ALU.add, op1=ALU.mult)
            else:
                nc.scalar.activation(out=y[pair][:, kind, :], in_=tile_acc[:], func=ACT.Identity,
                                     bias=bias_of(pair, kind), scale=1.0)

        def turn_back(pair):
            yt[pair] = yt_pool.tile([P, 2, B, DH], F32, name="yt")
            for kind in range(2):
                for b in range(B):
                    if pair < H and kind == 0:
                        nc.tensor.matmul(out=yt[pair][:, 0, b, :], lhsT=bm[pair][:, 0, b, :],
                                         rhs=ident[:], is_transpose=True, start=True, stop=False)
                        nc.tensor.matmul(out=yt[pair][:, 0, b, :], lhsT=bm[pair][:, 1, b, :],
                                         rhs=swap[:].rearrange("p i e -> p (i e)"), is_transpose=True,
                                         start=False, stop=True)
                    else:
                        nc.tensor.transpose(yt[pair][:, kind, b, :], y[pair][:, kind, b * T:(b + 1) * T], ident[:])
            ot[pair] = work.tile([P, B, 2, DH], F32, name="ot", bufs=4)
            if pair < H:
                nc.scalar.copy(out=ot[pair][:].rearrange("p b a (k c) -> p k (b a) c", k=2),
                               in_=yt[pair][:].rearrange("p k b (a c) -> p k (b a) c", a=2))
            else:
                nc.scalar.copy(out=ot[pair][:].rearrange("p b a c -> p a b c"), in_=yt[pair][:])
            j, h0 = pair // (H // 2), 2 * (pair % (H // 2))
            nc.sync.dma_start(out=outs[j][:, :, h0:h0 + 2, :], in_=ot[pair][:])

        wbs, planes, grps = {}, {}, {}

        def s_widen(k, j):
            h = S_GROUPS[k][j]
            wbs[h] = spath.tile([P, M], BF16, name="wbs", bufs=GS)
            nc.scalar.copy(out=wbs[h][:], in_=sbyte[h][:].bitcast(FP8))

        def s_planes(k, g, t0):
            if t0 == 0:
                planes[(k, g)] = spath.tile([P, 4, GS * P], BF16, name="planes")
            u = t0 // 2
            tpw = tp_pool.tile([P, GS, P], F32, name="tp")
            for j in range(GS):
                nc.tensor.transpose(tpw[:, j, :], wbs[S_GROUPS[k][j]][:].bitcast(F32)[:, 256 * g + u:256 * (g + 1):2],
                                    ident[:])
            both = tpw[:].rearrange("p j r -> p (j r)").bitcast(BF16).rearrange("p (c e) -> p c e", e=2)
            for e in range(2):
                nc.scalar.activation(out=planes[(k, g)][:, t0 + e, :], in_=both[:, :, e],
                                     func=ACT.Copy, scale=s_col[:, g, t0 + e:t0 + e + 1])

        def s_interleave(k, g):
            grps[(k, g)] = spath.tile([P, GS * P, 4], BF16, name="grps", align_bytes=64)
            if G * k + g in V_INTERLEAVES:
                nc.vector.tensor_copy(out=grps[(k, g)][:], in_=planes[(k, g)][:].rearrange("p t c -> p c t"))
            else:
                nc.scalar.copy(out=grps[(k, g)][:].rearrange("p (c i) t -> p c t i", i=4),
                               in_=planes[(k, g)][:].rearrange("p t (c i) -> p c t i", i=4))

        def s_quantize(k, g):
            codes = spath.tile([P, GS * P], U32, name="codes_s", bufs=2 * G, align_bytes=64)
            sc = spath.tile([P, GS * P], U8, name="sc_s", bufs=2 * G, align_bytes=64)
            nc.vector.quantize_mx(out=codes[:].bitcast(FP8X4), scales=sc[:],
                                  in_=grps[(k, g)][:].rearrange("p c t -> p (c t)"))
            for j in range(GS):
                h = S_GROUPS[k][j]
                lhs.setdefault((h // 2, h % 2), []).append((codes[:, j * P:(j + 1) * P], sc[:, j * P:(j + 1) * P]))

        background = []
        for k in range(len(S_GROUPS)):
            for j in range(GS):
                background.append(("widen", k, j))
            for g in range(G):
                background.append(("planes", k, g, 0))
                background.append(("planes", k, g, 2))
                background.append(("interleave", k, g))
        bg_at, quant_at, mult_at, back_at, squant_at = {}, {}, {}, {}, {}
        for s in range(1, NV, 2):
            quant_at[s + 2] = v_heads[s] // 2
            mult_at.setdefault(s + 3, []).append((v_heads[s] // 2, 0))
            mult_at.setdefault(s + 4, []).append((v_heads[s] // 2, 1))
            back_at.setdefault(s + 5, []).append(v_heads[s] // 2)
        for n in range(len(background)):
            task = background[n]
            s = (n * BG_STEPS) // len(background)
            bg_at.setdefault(s, []).append(task)
            if task[0] == "interleave":
                squant_at.setdefault(s + 1, []).append((task[1], task[2]))
                if task[2] == G - 1:
                    for j in range(GS):
                        mult_at.setdefault(s + 2 + j, []).append((S_GROUPS[task[1]][j] // 2, j % 2))
                        if j % 2 == 1:
                            back_at.setdefault(s + 3 + j, []).append(S_GROUPS[task[1]][j] // 2)
        last_step = max(back_at)

        for s in range(last_step + 1):
            if s + LOAD_AHEAD < NV:
                load(v_heads[s + LOAD_AHEAD])
            if 0 <= s - 1 < NV:
                turn(v_heads[s - 1])
            if s == 0:
                prepare_x()
            if s == 1:
                prepare_bias()
            if s < NV:
                widen(v_heads[s], 4 if s == 0 else 1)
            if s == 4:
                tables_rest(neg_turns)
            for pk in mult_at.get(s, []):
                multiply(pk[0], pk[1])
            for pair in back_at.get(s, []):
                turn_back(pair)
            if s == 2:
                quantize_x()
            if s in quant_at:
                quantize(quant_at[s])
            for task in bg_at.get(s, []):
                if task[0] == "widen":
                    s_widen(task[1], task[2])
                elif task[0] == "planes":
                    s_planes(task[1], task[2], task[3])
                else:
                    s_interleave(task[1], task[2])
            for kg in squant_at.get(s, []):
                s_quantize(kg[0], kg[1])
